import numpy as np
import ml_dtypes

BF16 = ml_dtypes.bfloat16


def bf(x):
    return np.asarray(x, np.float32).astype(BF16)


def f32(x):
    return np.asarray(x, np.float32)


def f64(x):
    return np.asarray(x).astype(np.float64)


def striped(idx):
    return np.tile(idx.reshape(-1, 16).T, (8, 1))


V, D, E, H, M, N = 2048, 128, 128, 128, 512, 1024


def sigmoid(v):
    return 1.0 / (1.0 + np.exp(-v))


def setup_inputs():
    return {
        "table": bf(np.random.standard_normal((D, V))),
        "w_emb": bf(0.6 * np.random.standard_normal((D, M)) / np.sqrt(D)),
        "ctx": bf(np.random.standard_normal((E, N))),
        "w_ctx": bf(0.6 * np.random.standard_normal((E, M)) / np.sqrt(E)),
        "h0": bf(np.random.standard_normal((H, N))),
        "w_hh": bf(0.6 * np.random.standard_normal((H, M)) / np.sqrt(H)),
        "b": f32(0.1 * np.random.standard_normal((M, 1))),
        "c0": f32(np.random.standard_normal((H, N))),
        "offs": striped(np.random.permutation(np.tile(np.arange(V), 2))[:N]),
    }


def reference(table, w_emb, ctx, w_ctx, h0, w_hh, b, c0, offs):
    idx = offs[:16].T.reshape(-1)
    pre = f64(w_emb).T @ f64(table)[:, idx] + f64(w_ctx).T @ f64(ctx) + f64(w_hh).T @ f64(h0) + f64(b)
    a_in, a_forget, a_cell, a_out = pre.reshape(-1, H, N)
    cell = sigmoid(a_forget) * f64(c0) + sigmoid(a_in) * np.tanh(a_cell)
    return sigmoid(a_out) * np.tanh(cell)

@@ -1,0 +1,78 @@
+import concourse.mybir as mybir
+
+BF16, F32, U16 = mybir.dt.bfloat16, mybir.dt.float32, mybir.dt.uint16
+SIGMOID, TANH = mybir.ActivationFunctionType.Sigmoid, mybir.ActivationFunctionType.Tanh
+MULT, ADD = mybir.AluOpType.mult, mybir.AluOpType.add
+
+P = 128
+V = 2048
+N = 1024
+PIECE = 512
+GATE_IN, GATE_FORGET, GATE_CANDIDATE, GATE_OUT = 0, 1, 2, 3
+GATES = 4
+
+FLOPS = 2 * 3 * P * GATES * P * N
+
+
+def tile_pgndecoder_kernel(tc, table, w_emb, ctx, w_ctx, h0, w_hh, b, c0, offs, out):
+    nc = tc.nc
+    with (
+        tc.tile_pool(name="held", bufs=1) as held,
+        tc.tile_pool(name="work", bufs=2) as work,
+        tc.psum_pool(name="psum", bufs=1) as psum,
+    ):
+        offsets = held.tile([P, N // 16], U16, name="offsets")
+        nc.sync.dma_start(offsets[:], offs)
+        w_ctx_sb = held.tile([P, GATES * P], BF16, name="w_ctx_sb")
+        nc.sync.dma_start(w_ctx_sb[:], w_ctx)
+        w_hh_sb = held.tile([P, GATES * P], BF16, name="w_hh_sb")
+        nc.scalar.dma_start(w_hh_sb[:], w_hh)
+        ctx_sb = held.tile([P, N], BF16, name="ctx_sb")
+        nc.sync.dma_start(ctx_sb[:], ctx)
+        h0_sb = held.tile([P, N], BF16, name="h0_sb")
+        nc.scalar.dma_start(h0_sb[:], h0)
+        table_sb = held.tile([P, V], BF16, name="table_sb")
+        nc.sync.dma_start(table_sb[:], table)
+        w_emb_sb = held.tile([P, GATES * P], BF16, name="w_emb_sb")
+        nc.scalar.dma_start(w_emb_sb[:], w_emb)
+        bias_sb = held.tile([P, GATES], F32, name="bias_sb")
+        with nc.allow_non_contiguous_dma(reason="512 bias values, one to a partition and gate"):
+            nc.gpsimd.dma_start(bias_sb[:], b.rearrange("(g p) o -> p (g o)", p=P))
+        c0_sb = held.tile([P, N], F32, name="c0_sb")
+        nc.gpsimd.dma_start(c0_sb[:], c0)
+
+        pre = [[psum.tile([P, PIECE], F32, name=f"pre{piece}_{g}") for g in range(GATES)] for piece in range(N // PIECE)]
+        for piece in range(N // PIECE):
+            cols = slice(piece * PIECE, (piece + 1) * PIECE)
+            for g in range(GATES):
+                rows = slice(g * P, (g + 1) * P)
+                nc.tensor.matmul(pre[piece][g][:], w_ctx_sb[:, rows], ctx_sb[:, cols], start=True, stop=False)
+                nc.tensor.matmul(pre[piece][g][:], w_hh_sb[:, rows], h0_sb[:, cols], start=False, stop=False)
+
+        for piece in range(N // PIECE):
+            cols = slice(piece * PIECE, (piece + 1) * PIECE)
+            piece_offsets = offsets[:, piece * (PIECE // 16) : (piece + 1) * (PIECE // 16)]
+
+            gate = []
+            for g in range(GATES):
+                rows = slice(g * P, (g + 1) * P)
+                nc.tensor.matmul(
+                    pre[piece][g][:], w_emb_sb[:, rows], table_sb[:].indirect(piece_offsets), start=False, stop=True
+                )
+                squashed = work.tile([P, PIECE], F32, name=f"gate{g}")
+                nc.scalar.activation(
+                    squashed[:], pre[piece][g][:], TANH if g == GATE_CANDIDATE else SIGMOID, bias=bias_sb[:, g : g + 1]
+                )
+                gate.append(squashed)
+
+            kept = work.tile([P, PIECE], F32, name="kept")
+            nc.vector.tensor_tensor(kept[:], gate[GATE_FORGET][:], c0_sb[:, cols], MULT)
+            fresh = work.tile([P, PIECE], F32, name="fresh")
+            nc.vector.tensor_tensor(fresh[:], gate[GATE_IN][:], gate[GATE_CANDIDATE][:], MULT)
+            cell = work.tile([P, PIECE], F32, name="cell")
+            nc.vector.tensor_tensor(cell[:], kept[:], fresh[:], ADD)
+            tanh_cell = work.tile([P, PIECE], F32, name="tanh_cell")
+            nc.scalar.activation(tanh_cell[:], cell[:], TANH)
+            hidden = work.tile([P, PIECE], F32, name="hidden")
+            nc.vector.tensor_tensor(hidden[:], gate[GATE_OUT][:], tanh_cell[:], MULT)
+            nc.sync.dma_start(out[:, cols], hidden[:])

@@ -21,35 +21,39 @@ def tile_pgndecoder_kernel(tc, table, w_emb, ctx, w_ctx, h0, w_hh, b, c0, offs, 
         tc.tile_pool(name="work", bufs=2) as work,
         tc.psum_pool(name="psum", bufs=1) as psum,
     ):
+        pieces = range(N // PIECE)
         offsets = held.tile([P, N // 16], U16, name="offsets")
-        nc.sync.dma_start(offsets[:], offs)
-        w_ctx_sb = held.tile([P, GATES * P], BF16, name="w_ctx_sb")
-        nc.sync.dma_start(w_ctx_sb[:], w_ctx)
-        w_hh_sb = held.tile([P, GATES * P], BF16, name="w_hh_sb")
-        nc.scalar.dma_start(w_hh_sb[:], w_hh)
-        ctx_sb = held.tile([P, N], BF16, name="ctx_sb")
-        nc.sync.dma_start(ctx_sb[:], ctx)
-        h0_sb = held.tile([P, N], BF16, name="h0_sb")
-        nc.scalar.dma_start(h0_sb[:], h0)
         table_sb = held.tile([P, V], BF16, name="table_sb")
-        nc.sync.dma_start(table_sb[:], table)
         w_emb_sb = held.tile([P, GATES * P], BF16, name="w_emb_sb")
-        nc.scalar.dma_start(w_emb_sb[:], w_emb)
+        w_ctx_sb = held.tile([P, GATES * P], BF16, name="w_ctx_sb")
+        w_hh_sb = held.tile([P, GATES * P], BF16, name="w_hh_sb")
+        ctx_sb = [held.tile([P, PIECE], BF16, name=f"ctx_sb{piece}") for piece in pieces]
+        h0_sb = [held.tile([P, PIECE], BF16, name=f"h0_sb{piece}") for piece in pieces]
+        c0_sb = [held.tile([P, PIECE], F32, name=f"c0_sb{piece}") for piece in pieces]
         bias_sb = held.tile([P, GATES], F32, name="bias_sb")
+
+        nc.sync.dma_start(w_ctx_sb[:], w_ctx)
+        nc.scalar.dma_start(ctx_sb[0][:], ctx[:, 0:PIECE])
+        nc.sync.dma_start(w_hh_sb[:], w_hh)
+        nc.scalar.dma_start(h0_sb[0][:], h0[:, 0:PIECE])
+        nc.sync.dma_start(ctx_sb[1][:], ctx[:, PIECE:N])
+        nc.scalar.dma_start(h0_sb[1][:], h0[:, PIECE:N])
+        nc.sync.dma_start(offsets[:], offs)
+        nc.scalar.dma_start(w_emb_sb[:], w_emb)
+        nc.sync.dma_start(table_sb[:], table)
+        nc.sync.dma_start(c0_sb[0][:], c0[:, 0:PIECE])
+        nc.sync.dma_start(c0_sb[1][:], c0[:, PIECE:N])
         with nc.allow_non_contiguous_dma(reason="512 bias values, one to a partition and gate"):
             nc.gpsimd.dma_start(bias_sb[:], b.rearrange("(g p) o -> p (g o)", p=P))
-        c0_sb = held.tile([P, N], F32, name="c0_sb")
-        nc.gpsimd.dma_start(c0_sb[:], c0)
 
-        pre = [[psum.tile([P, PIECE], F32, name=f"pre{piece}_{g}") for g in range(GATES)] for piece in range(N // PIECE)]
-        for piece in range(N // PIECE):
-            cols = slice(piece * PIECE, (piece + 1) * PIECE)
+        pre = [[psum.tile([P, PIECE], F32, name=f"pre{piece}_{g}") for g in range(GATES)] for piece in pieces]
+        for piece in pieces:
             for g in range(GATES):
                 rows = slice(g * P, (g + 1) * P)
-                nc.tensor.matmul(pre[piece][g][:], w_ctx_sb[:, rows], ctx_sb[:, cols], start=True, stop=False)
-                nc.tensor.matmul(pre[piece][g][:], w_hh_sb[:, rows], h0_sb[:, cols], start=False, stop=False)
+                nc.tensor.matmul(pre[piece][g][:], w_ctx_sb[:, rows], ctx_sb[piece][:], start=True, stop=False)
+                nc.tensor.matmul(pre[piece][g][:], w_hh_sb[:, rows], h0_sb[piece][:], start=False, stop=False)
 
-        for piece in range(N // PIECE):
+        for piece in pieces:
             cols = slice(piece * PIECE, (piece + 1) * PIECE)
             piece_offsets = offsets[:, piece * (PIECE // 16) : (piece + 1) * (PIECE // 16)]
 
@@ -66,7 +70,7 @@ def tile_pgndecoder_kernel(tc, table, w_emb, ctx, w_ctx, h0, w_hh, b, c0, offs, 
                 gate.append(squashed)
 
             kept = work.tile([P, PIECE], F32, name="kept")
-            nc.vector.tensor_tensor(kept[:], gate[GATE_FORGET][:], c0_sb[:, cols], MULT)
+            nc.vector.tensor_tensor(kept[:], gate[GATE_FORGET][:], c0_sb[piece][:], MULT)
             fresh = work.tile([P, PIECE], F32, name="fresh")
             nc.vector.tensor_tensor(fresh[:], gate[GATE_IN][:], gate[GATE_CANDIDATE][:], MULT)
             cell = work.tile([P, PIECE], F32, name="cell")

@@ -10,6 +10,7 @@ N = 1024
 PIECE = 512
 GATE_IN, GATE_FORGET, GATE_CANDIDATE, GATE_OUT = 0, 1, 2, 3
 GATES = 4
+WARM_UP_MATMULS = 6
 
 FLOPS = 2 * 3 * P * GATES * P * N
 
@@ -47,6 +48,12 @@ def tile_pgndecoder_kernel(tc, table, w_emb, ctx, w_ctx, h0, w_hh, b, c0, offs, 
             nc.gpsimd.dma_start(bias_sb[:], b.rearrange("(g p) o -> p (g o)", p=P))
 
         pre = [[psum.tile([P, PIECE], F32, name=f"pre{piece}_{g}") for g in range(GATES)] for piece in pieces]
+
+        zeros = held.tile([P, PIECE], BF16, name="zeros")
+        nc.vector.memset(zeros[:], 0.0)
+        for repeat in range(WARM_UP_MATMULS):
+            nc.tensor.matmul(pre[1][GATE_OUT][:], zeros[:, 0:P], zeros[:], start=True, stop=True)
+
         for piece in pieces:
             for g in range(GATES):
                 rows = slice(g * P, (g + 1) * P)

@@ -10,7 +10,8 @@ N = 1024
 PIECE = 512
 GATE_IN, GATE_FORGET, GATE_CANDIDATE, GATE_OUT = 0, 1, 2, 3
 GATES = 4
-WARM_UP_MATMULS = 6
+CELL_GATES = (GATE_IN, GATE_CANDIDATE, GATE_FORGET)
+WARM_UP_MATMULS = 3
 
 FLOPS = 2 * 3 * P * GATES * P * N
 
@@ -33,6 +34,9 @@ def tile_pgndecoder_kernel(tc, table, w_emb, ctx, w_ctx, h0, w_hh, b, c0, offs, 
         c0_sb = [held.tile([P, PIECE], F32, name=f"c0_sb{piece}") for piece in pieces]
         bias_sb = held.tile([P, GATES], F32, name="bias_sb")
 
+        zeros = held.tile([P, PIECE], BF16, name="zeros")
+        nc.gpsimd.memset(zeros[:], 0.0)
+
         nc.sync.dma_start(w_ctx_sb[:], w_ctx)
         nc.scalar.dma_start(ctx_sb[0][:], ctx[:, 0:PIECE])
         nc.sync.dma_start(w_hh_sb[:], w_hh)
@@ -49,41 +53,53 @@ def tile_pgndecoder_kernel(tc, table, w_emb, ctx, w_ctx, h0, w_hh, b, c0, offs, 
 
         pre = [[psum.tile([P, PIECE], F32, name=f"pre{piece}_{g}") for g in range(GATES)] for piece in pieces]
 
-        zeros = held.tile([P, PIECE], BF16, name="zeros")
-        nc.vector.memset(zeros[:], 0.0)
+        def plain_products(piece, g, opens):
+            rows = slice(g * P, (g + 1) * P)
+            nc.tensor.matmul(pre[piece][g][:], w_ctx_sb[:, rows], ctx_sb[piece][:], start=opens, stop=False)
+            nc.tensor.matmul(pre[piece][g][:], w_hh_sb[:, rows], h0_sb[piece][:], start=False, stop=not opens)
+
+        def looked_up_product(piece, g, opens):
+            rows = slice(g * P, (g + 1) * P)
+            piece_offsets = offsets[:, piece * (PIECE // 16) : (piece + 1) * (PIECE // 16)]
+            nc.tensor.matmul(
+                pre[piece][g][:], w_emb_sb[:, rows], table_sb[:].indirect(piece_offsets), start=opens, stop=not opens
+            )
+
+        def squash(piece, g):
+            squashed = work.tile([P, PIECE], F32, name=f"gate{g}")
+            nc.scalar.activation(
+                squashed[:], pre[piece][g][:], TANH if g == GATE_CANDIDATE else SIGMOID, bias=bias_sb[:, g : g + 1]
+            )
+            return squashed
+
         for repeat in range(WARM_UP_MATMULS):
             nc.tensor.matmul(pre[1][GATE_OUT][:], zeros[:, 0:P], zeros[:], start=True, stop=True)
 
         for piece in pieces:
-            for g in range(GATES):
-                rows = slice(g * P, (g + 1) * P)
-                nc.tensor.matmul(pre[piece][g][:], w_ctx_sb[:, rows], ctx_sb[piece][:], start=True, stop=False)
-                nc.tensor.matmul(pre[piece][g][:], w_hh_sb[:, rows], h0_sb[piece][:], start=False, stop=False)
+            for g in CELL_GATES:
+                plain_products(piece, g, opens=True)
+        for piece in pieces:
+            for g in CELL_GATES:
+                looked_up_product(piece, g, opens=False)
+        for piece in pieces:
+            looked_up_product(piece, GATE_OUT, opens=True)
+        for piece in pieces:
+            plain_products(piece, GATE_OUT, opens=False)
+
+        cell = []
+        for piece in pieces:
+            gate_in, gate_candidate, gate_forget = [squash(piece, g) for g in CELL_GATES]
+            fresh = work.tile([P, PIECE], F32, name="fresh")
+            nc.vector.tensor_tensor(fresh[:], gate_in[:], gate_candidate[:], MULT)
+            kept = work.tile([P, PIECE], F32, name="kept")
+            nc.vector.tensor_tensor(kept[:], gate_forget[:], c0_sb[piece][:], MULT)
+            cell.append(work.tile([P, PIECE], F32, name="cell"))
+            nc.vector.tensor_tensor(cell[piece][:], kept[:], fresh[:], ADD)
 
         for piece in pieces:
-            cols = slice(piece * PIECE, (piece + 1) * PIECE)
-            piece_offsets = offsets[:, piece * (PIECE // 16) : (piece + 1) * (PIECE // 16)]
-
-            gate = []
-            for g in range(GATES):
-                rows = slice(g * P, (g + 1) * P)
-                nc.tensor.matmul(
-                    pre[piece][g][:], w_emb_sb[:, rows], table_sb[:].indirect(piece_offsets), start=False, stop=True
-                )
-                squashed = work.tile([P, PIECE], F32, name=f"gate{g}")
-                nc.scalar.activation(
-                    squashed[:], pre[piece][g][:], TANH if g == GATE_CANDIDATE else SIGMOID, bias=bias_sb[:, g : g + 1]
-                )
-                gate.append(squashed)
-
-            kept = work.tile([P, PIECE], F32, name="kept")
-            nc.vector.tensor_tensor(kept[:], gate[GATE_FORGET][:], c0_sb[piece][:], MULT)
-            fresh = work.tile([P, PIECE], F32, name="fresh")
-            nc.vector.tensor_tensor(fresh[:], gate[GATE_IN][:], gate[GATE_CANDIDATE][:], MULT)
-            cell = work.tile([P, PIECE], F32, name="cell")
-            nc.vector.tensor_tensor(cell[:], kept[:], fresh[:], ADD)
             tanh_cell = work.tile([P, PIECE], F32, name="tanh_cell")
-            nc.scalar.activation(tanh_cell[:], cell[:], TANH)
+            nc.scalar.activation(tanh_cell[:], cell[piece][:], TANH)
+            gate_out = squash(piece, GATE_OUT)
             hidden = work.tile([P, PIECE], F32, name="hidden")
-            nc.vector.tensor_tensor(hidden[:], gate[GATE_OUT][:], tanh_cell[:], MULT)
-            nc.sync.dma_start(out[:, cols], hidden[:])
+            nc.vector.tensor_tensor(hidden[:], gate_out[:], tanh_cell[:], MULT)
+            nc.sync.dma_start(out[:, piece * PIECE : (piece + 1) * PIECE], hidden[:])

@@ -11,6 +11,7 @@ PIECE = 512
 GATE_IN, GATE_FORGET, GATE_CANDIDATE, GATE_OUT = 0, 1, 2, 3
 GATES = 4
 CELL_GATES = (GATE_IN, GATE_CANDIDATE, GATE_FORGET)
+CUTS = (((0, PIECE),), ((0, PIECE // 2), (PIECE // 2, PIECE)))
 WARM_UP_MATMULS = 3
 
 FLOPS = 2 * 3 * P * GATES * P * N
@@ -21,6 +22,7 @@ def tile_pgndecoder_kernel(tc, table, w_emb, ctx, w_ctx, h0, w_hh, b, c0, offs, 
     with (
         tc.tile_pool(name="held", bufs=1) as held,
         tc.tile_pool(name="work", bufs=2) as work,
+        tc.tile_pool(name="tail", bufs=3) as tail,
         tc.psum_pool(name="psum", bufs=1) as psum,
     ):
         pieces = range(N // PIECE)
@@ -86,20 +88,30 @@ def tile_pgndecoder_kernel(tc, table, w_emb, ctx, w_ctx, h0, w_hh, b, c0, offs, 
         for piece in pieces:
             plain_products(piece, GATE_OUT, opens=False)
 
-        cell = []
+        cell = {}
         for piece in pieces:
             gate_in, gate_candidate, gate_forget = [squash(piece, g) for g in CELL_GATES]
-            fresh = work.tile([P, PIECE], F32, name="fresh")
-            nc.vector.tensor_tensor(fresh[:], gate_in[:], gate_candidate[:], MULT)
-            kept = work.tile([P, PIECE], F32, name="kept")
-            nc.vector.tensor_tensor(kept[:], gate_forget[:], c0_sb[piece][:], MULT)
-            cell.append(work.tile([P, PIECE], F32, name="cell"))
-            nc.vector.tensor_tensor(cell[piece][:], kept[:], fresh[:], ADD)
+            for lo, hi in CUTS[piece]:
+                fresh = tail.tile([P, hi - lo], F32, name="fresh")
+                nc.vector.tensor_tensor(fresh[:], gate_in[:, lo:hi], gate_candidate[:, lo:hi], MULT)
+                kept = tail.tile([P, hi - lo], F32, name="kept")
+                nc.vector.tensor_tensor(kept[:], gate_forget[:, lo:hi], c0_sb[piece][:, lo:hi], MULT)
+                cell[piece, lo] = tail.tile([P, hi - lo], F32, name="cell")
+                nc.vector.tensor_tensor(cell[piece, lo][:], kept[:], fresh[:], ADD)
+
+        tanh_cell = {}
+
+        def tanh_of_cell(piece):
+            for lo, hi in CUTS[piece]:
+                tanh_cell[piece, lo] = tail.tile([P, hi - lo], F32, name="tanh_cell")
+                nc.scalar.activation(tanh_cell[piece, lo][:], cell[piece, lo][:], TANH)
+
+        tanh_of_cell(0)
+        gate_out = [squash(piece, GATE_OUT) for piece in pieces]
+        tanh_of_cell(1)
 
         for piece in pieces:
-            tanh_cell = work.tile([P, PIECE], F32, name="tanh_cell")
-            nc.scalar.activation(tanh_cell[:], cell[piece][:], TANH)
-            gate_out = squash(piece, GATE_OUT)
-            hidden = work.tile([P, PIECE], F32, name="hidden")
-            nc.vector.tensor_tensor(hidden[:], gate_out[:], tanh_cell[:], MULT)
-            nc.sync.dma_start(out[:, piece * PIECE : (piece + 1) * PIECE], hidden[:])
+            for lo, hi in CUTS[piece]:
+                hidden = tail.tile([P, hi - lo], F32, name="hidden")
+                nc.vector.tensor_tensor(hidden[:], gate_out[piece][:, lo:hi], tanh_cell[piece, lo][:], MULT)
+                nc.sync.dma_start(out[:, piece * PIECE + lo : piece * PIECE + hi], hidden[:])

@@ -12,7 +12,6 @@ GATE_IN, GATE_FORGET, GATE_CANDIDATE, GATE_OUT = 0, 1, 2, 3
 GATES = 4
 CELL_GATES = (GATE_IN, GATE_CANDIDATE, GATE_FORGET)
 CUTS = (((0, PIECE),), ((0, PIECE // 2), (PIECE // 2, PIECE)))
-WARM_UP_MATMULS = 3
 
 FLOPS = 2 * 3 * P * GATES * P * N
 
@@ -35,9 +34,6 @@ def tile_pgndecoder_kernel(tc, table, w_emb, ctx, w_ctx, h0, w_hh, b, c0, offs, 
         h0_sb = [held.tile([P, PIECE], BF16, name=f"h0_sb{piece}") for piece in pieces]
         c0_sb = [held.tile([P, PIECE], F32, name=f"c0_sb{piece}") for piece in pieces]
         bias_sb = held.tile([P, GATES], F32, name="bias_sb")
-
-        zeros = held.tile([P, PIECE], BF16, name="zeros")
-        nc.gpsimd.memset(zeros[:], 0.0)
 
         nc.sync.dma_start(w_ctx_sb[:], w_ctx)
         nc.scalar.dma_start(ctx_sb[0][:], ctx[:, 0:PIECE])
@@ -73,9 +69,6 @@ def tile_pgndecoder_kernel(tc, table, w_emb, ctx, w_ctx, h0, w_hh, b, c0, offs, 
                 squashed[:], pre[piece][g][:], TANH if g == GATE_CANDIDATE else SIGMOID, bias=bias_sb[:, g : g + 1]
             )
             return squashed
-
-        for repeat in range(WARM_UP_MATMULS):
-            nc.tensor.matmul(pre[1][GATE_OUT][:], zeros[:, 0:P], zeros[:], start=True, stop=True)
 
         for piece in pieces:
             for g in CELL_GATES:

@@ -12,6 +12,7 @@ GATE_IN, GATE_FORGET, GATE_CANDIDATE, GATE_OUT = 0, 1, 2, 3
 GATES = 4
 CELL_GATES = (GATE_IN, GATE_CANDIDATE, GATE_FORGET)
 CUTS = (((0, PIECE),), ((0, PIECE // 2), (PIECE // 2, PIECE)))
+WARM_UP_MATMULS = 16
 
 FLOPS = 2 * 3 * P * GATES * P * N
 
@@ -34,6 +35,9 @@ def tile_pgndecoder_kernel(tc, table, w_emb, ctx, w_ctx, h0, w_hh, b, c0, offs, 
         h0_sb = [held.tile([P, PIECE], BF16, name=f"h0_sb{piece}") for piece in pieces]
         c0_sb = [held.tile([P, PIECE], F32, name=f"c0_sb{piece}") for piece in pieces]
         bias_sb = held.tile([P, GATES], F32, name="bias_sb")
+
+        zeros = held.tile([P, P], BF16, name="zeros")
+        nc.gpsimd.memset(zeros[:], 0.0)
 
         nc.sync.dma_start(w_ctx_sb[:], w_ctx)
         nc.scalar.dma_start(ctx_sb[0][:], ctx[:, 0:PIECE])
@@ -69,6 +73,9 @@ def tile_pgndecoder_kernel(tc, table, w_emb, ctx, w_ctx, h0, w_hh, b, c0, offs, 
                 squashed[:], pre[piece][g][:], TANH if g == GATE_CANDIDATE else SIGMOID, bias=bias_sb[:, g : g + 1]
             )
             return squashed
+
+        for repeat in range(WARM_UP_MATMULS):
+            nc.tensor.matmul(pre[1][GATE_OUT][:, 0:P], zeros[:], zeros[:], start=True, stop=True)
 
         for piece in pieces:
             for g in CELL_GATES:

@@ -8,6 +8,7 @@ P = 128
 V = 2048
 N = 1024
 PIECE = 512
+PLAIN = 128
 GATE_IN, GATE_FORGET, GATE_CANDIDATE, GATE_OUT = 0, 1, 2, 3
 GATES = 4
 CELL_GATES = (GATE_IN, GATE_CANDIDATE, GATE_FORGET)
@@ -43,22 +44,33 @@ def tile_pgndecoder_kernel(tc, table, w_emb, ctx, w_ctx, h0, w_hh, b, c0, offs, 
         nc.scalar.dma_start(ctx_sb[0][:], ctx[:, 0:PIECE])
         nc.sync.dma_start(w_hh_sb[:], w_hh)
         nc.scalar.dma_start(h0_sb[0][:], h0[:, 0:PIECE])
-        nc.sync.dma_start(ctx_sb[1][:], ctx[:, PIECE:N])
-        nc.scalar.dma_start(h0_sb[1][:], h0[:, PIECE:N])
+        with nc.allow_non_contiguous_dma(reason="512 bias values, one to a partition and gate"):
+            nc.scalar.dma_start(bias_sb[:], b.rearrange("(g p) o -> p (g o)", p=P))
         nc.sync.dma_start(offsets[:], offs)
         nc.scalar.dma_start(w_emb_sb[:], w_emb)
         nc.sync.dma_start(table_sb[:], table)
+        nc.scalar.dma_start(ctx_sb[1][:], ctx[:, PIECE:N])
+        nc.scalar.dma_start(h0_sb[1][:], h0[:, PIECE:N])
         nc.sync.dma_start(c0_sb[0][:], c0[:, 0:PIECE])
         nc.sync.dma_start(c0_sb[1][:], c0[:, PIECE:N])
-        with nc.allow_non_contiguous_dma(reason="512 bias values, one to a partition and gate"):
-            nc.gpsimd.dma_start(bias_sb[:], b.rearrange("(g p) o -> p (g o)", p=P))
 
         pre = [[psum.tile([P, PIECE], F32, name=f"pre{piece}_{g}") for g in range(GATES)] for piece in pieces]
 
         def plain_products(piece, g, opens):
             rows = slice(g * P, (g + 1) * P)
-            nc.tensor.matmul(pre[piece][g][:], w_ctx_sb[:, rows], ctx_sb[piece][:], start=opens, stop=False)
-            nc.tensor.matmul(pre[piece][g][:], w_hh_sb[:, rows], h0_sb[piece][:], start=False, stop=not opens)
+            steps = [
+                (weights, moving, lo)
+                for weights, moving in ((w_ctx_sb, ctx_sb[piece]), (w_hh_sb, h0_sb[piece]))
+                for lo in range(0, PIECE, PLAIN)
+            ]
+            for step, (weights, moving, lo) in enumerate(steps):
+                nc.tensor.matmul(
+                    pre[piece][g][:, lo : lo + PLAIN],
+                    weights[:, rows],
+                    moving[:, lo : lo + PLAIN],
+                    start=opens and step == 0,
+                    stop=not opens and step == len(steps) - 1,
+                )
 
         def looked_up_product(piece, g, opens):
             rows = slice(g * P, (g + 1) * P)
@@ -77,18 +89,28 @@ def tile_pgndecoder_kernel(tc, table, w_emb, ctx, w_ctx, h0, w_hh, b, c0, offs, 
         for repeat in range(WARM_UP_MATMULS):
             nc.tensor.matmul(pre[1][GATE_OUT][:, 0:P], zeros[:], zeros[:], start=True, stop=True)
 
-        for piece in pieces:
-            for g in CELL_GATES:
-                plain_products(piece, g, opens=True)
-        for piece in pieces:
-            for g in CELL_GATES:
-                looked_up_product(piece, g, opens=False)
-        for piece in pieces:
-            looked_up_product(piece, GATE_OUT, opens=True)
-        for piece in pieces:
-            plain_products(piece, GATE_OUT, opens=False)
+        for g in CELL_GATES:
+            plain_products(0, g, opens=True)
+        for g in CELL_GATES:
+            looked_up_product(0, g, opens=False)
+        for g in CELL_GATES:
+            looked_up_product(1, g, opens=True)
+        for g in CELL_GATES:
+            plain_products(1, g, opens=False)
+        plain_products(0, GATE_OUT, opens=True)
+        looked_up_product(0, GATE_OUT, opens=False)
+        looked_up_product(1, GATE_OUT, opens=True)
+        plain_products(1, GATE_OUT, opens=False)
 
         cell = {}
+        tanh_cell = {}
+
+        def tanh_of_cell(piece):
+            for lo, hi in CUTS[piece]:
+                tanh_cell[piece, lo] = tail.tile([P, hi - lo], F32, name="tanh_cell")
+                nc.scalar.activation(tanh_cell[piece, lo][:], cell[piece, lo][:], TANH)
+
+        gate_out = {}
         for piece in pieces:
             gate_in, gate_candidate, gate_forget = [squash(piece, g) for g in CELL_GATES]
             for lo, hi in CUTS[piece]:
@@ -98,17 +120,10 @@ def tile_pgndecoder_kernel(tc, table, w_emb, ctx, w_ctx, h0, w_hh, b, c0, offs, 
                 nc.vector.tensor_tensor(kept[:], gate_forget[:, lo:hi], c0_sb[piece][:, lo:hi], MULT)
                 cell[piece, lo] = tail.tile([P, hi - lo], F32, name="cell")
                 nc.vector.tensor_tensor(cell[piece, lo][:], kept[:], fresh[:], ADD)
-
-        tanh_cell = {}
-
-        def tanh_of_cell(piece):
-            for lo, hi in CUTS[piece]:
-                tanh_cell[piece, lo] = tail.tile([P, hi - lo], F32, name="tanh_cell")
-                nc.scalar.activation(tanh_cell[piece, lo][:], cell[piece, lo][:], TANH)
-
-        tanh_of_cell(0)
-        gate_out = [squash(piece, GATE_OUT) for piece in pieces]
-        tanh_of_cell(1)
+            if piece == 1:
+                gate_out[0] = squash(0, GATE_OUT)
+            tanh_of_cell(piece)
+        gate_out[1] = squash(1, GATE_OUT)
 
         for piece in pieces:
             for lo, hi in CUTS[piece]:

@@ -12,7 +12,9 @@ PLAIN = 128
 GATE_IN, GATE_FORGET, GATE_CANDIDATE, GATE_OUT = 0, 1, 2, 3
 GATES = 4
 CELL_GATES = (GATE_IN, GATE_CANDIDATE, GATE_FORGET)
-CUTS = (((0, PIECE),), ((0, PIECE // 2), (PIECE // 2, PIECE)))
+FIRST, SECOND = (0, PIECE), (PIECE, N)
+SECOND_HALVES = ((PIECE, PIECE + PIECE // 2), (PIECE + PIECE // 2, N))
+CUTS = {FIRST: (FIRST,), SECOND: SECOND_HALVES}
 WARM_UP_MATMULS = 16
 
 FLOPS = 2 * 3 * P * GATES * P * N
@@ -22,20 +24,20 @@ def tile_pgndecoder_kernel(tc, table, w_emb, ctx, w_ctx, h0, w_hh, b, c0, offs, 
     nc = tc.nc
     with (
         tc.tile_pool(name="held", bufs=1) as held,
-        tc.tile_pool(name="work", bufs=2) as work,
-        tc.tile_pool(name="tail", bufs=3) as tail,
         tc.psum_pool(name="psum", bufs=1) as psum,
     ):
-        pieces = range(N // PIECE)
         offsets = held.tile([P, N // 16], U16, name="offsets")
         table_sb = held.tile([P, V], BF16, name="table_sb")
         w_emb_sb = held.tile([P, GATES * P], BF16, name="w_emb_sb")
         w_ctx_sb = held.tile([P, GATES * P], BF16, name="w_ctx_sb")
         w_hh_sb = held.tile([P, GATES * P], BF16, name="w_hh_sb")
-        ctx_sb = [held.tile([P, PIECE], BF16, name=f"ctx_sb{piece}") for piece in pieces]
-        h0_sb = [held.tile([P, PIECE], BF16, name=f"h0_sb{piece}") for piece in pieces]
-        c0_sb = [held.tile([P, PIECE], F32, name=f"c0_sb{piece}") for piece in pieces]
+        ctx_sb = [held.tile([P, PIECE], BF16, name=f"ctx_sb{lo}") for lo, hi in (FIRST, SECOND)]
+        h0_sb = [held.tile([P, PIECE], BF16, name=f"h0_sb{lo}") for lo, hi in (FIRST, SECOND)]
+        c0_sb = [held.tile([P, PIECE], F32, name=f"c0_sb{lo}") for lo, hi in (FIRST, SECOND)]
         bias_sb = held.tile([P, GATES], F32, name="bias_sb")
+
+        def columns(piece_tiles, lo, hi):
+            return piece_tiles[lo // PIECE][:, lo % PIECE : lo % PIECE + hi - lo]
 
         zeros = held.tile([P, P], BF16, name="zeros")
         nc.gpsimd.memset(zeros[:], 0.0)
@@ -54,79 +56,94 @@ def tile_pgndecoder_kernel(tc, table, w_emb, ctx, w_ctx, h0, w_hh, b, c0, offs, 
         nc.sync.dma_start(c0_sb[0][:], c0[:, 0:PIECE])
         nc.sync.dma_start(c0_sb[1][:], c0[:, PIECE:N])
 
-        pre = [[psum.tile([P, PIECE], F32, name=f"pre{piece}_{g}") for g in range(GATES)] for piece in pieces]
+        pre = {(g, lo): psum.tile([P, hi - lo], F32, name=f"pre{g}_{lo}") for g in CELL_GATES for lo, hi in (FIRST, SECOND)}
+        for lo, hi in SECOND_HALVES:
+            pre[GATE_OUT, lo] = psum.tile([P, hi - lo], F32, name=f"pre{GATE_OUT}_{lo}")
 
-        def plain_products(piece, g, opens):
+        def plain_products(g, lo, hi, opens):
             rows = slice(g * P, (g + 1) * P)
             steps = [
-                (weights, moving, lo)
-                for weights, moving in ((w_ctx_sb, ctx_sb[piece]), (w_hh_sb, h0_sb[piece]))
-                for lo in range(0, PIECE, PLAIN)
+                (weights, moving, at)
+                for weights, moving in ((w_ctx_sb, ctx_sb), (w_hh_sb, h0_sb))
+                for at in range(lo, hi, PLAIN)
             ]
-            for step, (weights, moving, lo) in enumerate(steps):
+            for step, (weights, moving, at) in enumerate(steps):
                 nc.tensor.matmul(
-                    pre[piece][g][:, lo : lo + PLAIN],
+                    pre[g, lo][:, at - lo : at - lo + PLAIN],
                     weights[:, rows],
-                    moving[:, lo : lo + PLAIN],
+                    columns(moving, at, at + PLAIN),
                     start=opens and step == 0,
                     stop=not opens and step == len(steps) - 1,
                 )
 
-        def looked_up_product(piece, g, opens):
+        def looked_up_product(g, lo, hi, opens):
             rows = slice(g * P, (g + 1) * P)
-            piece_offsets = offsets[:, piece * (PIECE // 16) : (piece + 1) * (PIECE // 16)]
             nc.tensor.matmul(
-                pre[piece][g][:], w_emb_sb[:, rows], table_sb[:].indirect(piece_offsets), start=opens, stop=not opens
+                pre[g, lo][:],
+                w_emb_sb[:, rows],
+                table_sb[:].indirect(offsets[:, lo // 16 : hi // 16]),
+                start=opens,
+                stop=not opens,
             )
 
-        def squash(piece, g):
-            squashed = work.tile([P, PIECE], F32, name=f"gate{g}")
+        def squash(g, lo, hi):
+            squashed = held.tile([P, hi - lo], F32, name=f"gate{g}_{lo}")
             nc.scalar.activation(
-                squashed[:], pre[piece][g][:], TANH if g == GATE_CANDIDATE else SIGMOID, bias=bias_sb[:, g : g + 1]
+                squashed[:], pre[g, lo][:], TANH if g == GATE_CANDIDATE else SIGMOID, bias=bias_sb[:, g : g + 1]
             )
             return squashed
-
-        for repeat in range(WARM_UP_MATMULS):
-            nc.tensor.matmul(pre[1][GATE_OUT][:, 0:P], zeros[:], zeros[:], start=True, stop=True)
-
-        for g in CELL_GATES:
-            plain_products(0, g, opens=True)
-        for g in CELL_GATES:
-            looked_up_product(0, g, opens=False)
-        for g in CELL_GATES:
-            looked_up_product(1, g, opens=True)
-        for g in CELL_GATES:
-            plain_products(1, g, opens=False)
-        plain_products(0, GATE_OUT, opens=True)
-        looked_up_product(0, GATE_OUT, opens=False)
-        looked_up_product(1, GATE_OUT, opens=True)
-        plain_products(1, GATE_OUT, opens=False)
 
         cell = {}
         tanh_cell = {}
 
-        def tanh_of_cell(piece):
+        def new_cell_state(piece):
+            start = piece[0]
+            gate_in, gate_candidate, gate_forget = [squash(g, *piece) for g in CELL_GATES]
             for lo, hi in CUTS[piece]:
-                tanh_cell[piece, lo] = tail.tile([P, hi - lo], F32, name="tanh_cell")
-                nc.scalar.activation(tanh_cell[piece, lo][:], cell[piece, lo][:], TANH)
+                cut = slice(lo - start, hi - start)
+                fresh = held.tile([P, hi - lo], F32, name=f"fresh{lo}")
+                nc.vector.tensor_tensor(fresh[:], gate_in[:, cut], gate_candidate[:, cut], MULT)
+                kept = held.tile([P, hi - lo], F32, name=f"kept{lo}")
+                nc.vector.tensor_tensor(kept[:], gate_forget[:, cut], columns(c0_sb, lo, hi), MULT)
+                cell[lo] = held.tile([P, hi - lo], F32, name=f"cell{lo}")
+                nc.vector.tensor_tensor(cell[lo][:], kept[:], fresh[:], ADD)
 
-        gate_out = {}
-        for piece in pieces:
-            gate_in, gate_candidate, gate_forget = [squash(piece, g) for g in CELL_GATES]
-            for lo, hi in CUTS[piece]:
-                fresh = tail.tile([P, hi - lo], F32, name="fresh")
-                nc.vector.tensor_tensor(fresh[:], gate_in[:, lo:hi], gate_candidate[:, lo:hi], MULT)
-                kept = tail.tile([P, hi - lo], F32, name="kept")
-                nc.vector.tensor_tensor(kept[:], gate_forget[:, lo:hi], c0_sb[piece][:, lo:hi], MULT)
-                cell[piece, lo] = tail.tile([P, hi - lo], F32, name="cell")
-                nc.vector.tensor_tensor(cell[piece, lo][:], kept[:], fresh[:], ADD)
-            if piece == 1:
-                gate_out[0] = squash(0, GATE_OUT)
-            tanh_of_cell(piece)
-        gate_out[1] = squash(1, GATE_OUT)
+        def tanh_of_cell(lo, hi):
+            tanh_cell[lo] = held.tile([P, hi - lo], F32, name=f"tanh_cell{lo}")
+            nc.scalar.activation(tanh_cell[lo][:], cell[lo][:], TANH)
 
-        for piece in pieces:
-            for lo, hi in CUTS[piece]:
-                hidden = tail.tile([P, hi - lo], F32, name="hidden")
-                nc.vector.tensor_tensor(hidden[:], gate_out[piece][:, lo:hi], tanh_cell[piece, lo][:], MULT)
-                nc.sync.dma_start(out[:, piece * PIECE + lo : piece * PIECE + hi], hidden[:])
+        def new_hidden_state(gate_out, lo, hi):
+            hidden = held.tile([P, hi - lo], F32, name=f"hidden{lo}")
+            nc.vector.tensor_tensor(hidden[:], gate_out[:], tanh_cell[lo][:], MULT)
+            nc.sync.dma_start(out[:, lo:hi], hidden[:])
+
+        last_bank = pre[GATE_OUT, SECOND_HALVES[1][0]]
+        for repeat in range(WARM_UP_MATMULS):
+            nc.tensor.matmul(last_bank[:, 0:P], zeros[:], zeros[:], start=True, stop=True)
+
+        for g in CELL_GATES:
+            plain_products(g, *FIRST, opens=True)
+        for g in CELL_GATES:
+            looked_up_product(g, *FIRST, opens=False)
+        for g in CELL_GATES:
+            looked_up_product(g, *SECOND, opens=True)
+        new_cell_state(FIRST)
+        tanh_of_cell(*FIRST)
+
+        for g in CELL_GATES:
+            plain_products(g, *SECOND, opens=False)
+        pre[GATE_OUT, 0] = psum.tile([P, PIECE], F32, name=f"pre{GATE_OUT}_0", tag=f"pre{GATE_IN}_0")
+        plain_products(GATE_OUT, *FIRST, opens=True)
+        new_cell_state(SECOND)
+
+        looked_up_product(GATE_OUT, *FIRST, opens=False)
+        for half in SECOND_HALVES:
+            looked_up_product(GATE_OUT, *half, opens=True)
+        for half in SECOND_HALVES:
+            plain_products(GATE_OUT, *half, opens=False)
+
+        new_hidden_state(squash(GATE_OUT, *FIRST), *FIRST)
+        for half in SECOND_HALVES:
+            tanh_of_cell(*half)
+        for half in SECOND_HALVES:
+            new_hidden_state(squash(GATE_OUT, *half), *half)

@@ -57,8 +57,8 @@ def tile_pgndecoder_kernel(tc, table, w_emb, ctx, w_ctx, h0, w_hh, b, c0, offs, 
         nc.sync.dma_start(c0_sb[1][:], c0[:, PIECE:N])
 
         pre = {(g, lo): psum.tile([P, hi - lo], F32, name=f"pre{g}_{lo}") for g in CELL_GATES for lo, hi in (FIRST, SECOND)}
-        for lo, hi in SECOND_HALVES:
-            pre[GATE_OUT, lo] = psum.tile([P, hi - lo], F32, name=f"pre{GATE_OUT}_{lo}")
+        pre[GATE_OUT, 0] = psum.tile([P, PIECE], F32, name=f"pre{GATE_OUT}_0")
+        pre[GATE_OUT, PIECE] = psum.tile([P, PIECE // 2], F32, name=f"pre{GATE_OUT}_{PIECE}")
 
         def plain_products(g, lo, hi, opens):
             rows = slice(g * P, (g + 1) * P)
@@ -117,11 +117,10 @@ def tile_pgndecoder_kernel(tc, table, w_emb, ctx, w_ctx, h0, w_hh, b, c0, offs, 
             nc.vector.tensor_tensor(hidden[:], gate_out[:], tanh_cell[lo][:], MULT)
             nc.sync.dma_start(out[:, lo:hi], hidden[:])
 
-        last_bank = pre[GATE_OUT, SECOND_HALVES[1][0]]
         for repeat in range(WARM_UP_MATMULS):
-            nc.tensor.matmul(last_bank[:, 0:P], zeros[:], zeros[:], start=True, stop=True)
+            nc.tensor.matmul(pre[GATE_OUT, PIECE][:, 0:P], zeros[:], zeros[:], start=True, stop=True)
 
-        for g in CELL_GATES:
+        for g in CELL_GATES + (GATE_OUT,):
             plain_products(g, *FIRST, opens=True)
         for g in CELL_GATES:
             looked_up_product(g, *FIRST, opens=False)
@@ -132,10 +131,10 @@ def tile_pgndecoder_kernel(tc, table, w_emb, ctx, w_ctx, h0, w_hh, b, c0, offs, 
 
         for g in CELL_GATES:
             plain_products(g, *SECOND, opens=False)
-        pre[GATE_OUT, 0] = psum.tile([P, PIECE], F32, name=f"pre{GATE_OUT}_0", tag=f"pre{GATE_IN}_0")
-        plain_products(GATE_OUT, *FIRST, opens=True)
         new_cell_state(SECOND)
 
+        last_lo, last_hi = SECOND_HALVES[1]
+        pre[GATE_OUT, last_lo] = psum.tile([P, last_hi - last_lo], F32, name=f"pre{GATE_OUT}_{last_lo}", tag=f"pre{GATE_IN}_0")
         looked_up_product(GATE_OUT, *FIRST, opens=False)
         for half in SECOND_HALVES:
             looked_up_product(GATE_OUT, *half, opens=True)

@@ -46,14 +46,14 @@ def tile_pgndecoder_kernel(tc, table, w_emb, ctx, w_ctx, h0, w_hh, b, c0, offs, 
         nc.scalar.dma_start(ctx_sb[0][:], ctx[:, 0:PIECE])
         nc.sync.dma_start(w_hh_sb[:], w_hh)
         nc.scalar.dma_start(h0_sb[0][:], h0[:, 0:PIECE])
-        with nc.allow_non_contiguous_dma(reason="512 bias values, one to a partition and gate"):
-            nc.scalar.dma_start(bias_sb[:], b.rearrange("(g p) o -> p (g o)", p=P))
         nc.sync.dma_start(offsets[:], offs)
         nc.scalar.dma_start(w_emb_sb[:], w_emb)
         nc.sync.dma_start(table_sb[:], table)
-        nc.scalar.dma_start(ctx_sb[1][:], ctx[:, PIECE:N])
-        nc.scalar.dma_start(h0_sb[1][:], h0[:, PIECE:N])
+        with nc.allow_non_contiguous_dma(reason="512 bias values, one to a partition and gate"):
+            nc.scalar.dma_start(bias_sb[:], b.rearrange("(g p) o -> p (g o)", p=P))
         nc.sync.dma_start(c0_sb[0][:], c0[:, 0:PIECE])
+        nc.sync.dma_start(ctx_sb[1][:], ctx[:, PIECE:N])
+        nc.sync.dma_start(h0_sb[1][:], h0[:, PIECE:N])
         nc.sync.dma_start(c0_sb[1][:], c0[:, PIECE:N])
 
         pre = {(g, lo): psum.tile([P, hi - lo], F32, name=f"pre{g}_{lo}") for g in CELL_GATES for lo, hi in (FIRST, SECOND)}

@@ -8,7 +8,7 @@ P = 128
 V = 2048
 N = 1024
 PIECE = 512
-PLAIN = 128
+NARROW = 128
 GATE_IN, GATE_FORGET, GATE_CANDIDATE, GATE_OUT = 0, 1, 2, 3
 GATES = 4
 CELL_GATES = (GATE_IN, GATE_CANDIDATE, GATE_FORGET)
@@ -60,18 +60,18 @@ def tile_pgndecoder_kernel(tc, table, w_emb, ctx, w_ctx, h0, w_hh, b, c0, offs, 
         pre[GATE_OUT, 0] = psum.tile([P, PIECE], F32, name=f"pre{GATE_OUT}_0")
         pre[GATE_OUT, PIECE] = psum.tile([P, PIECE // 2], F32, name=f"pre{GATE_OUT}_{PIECE}")
 
-        def plain_products(g, lo, hi, opens):
+        def plain_products(g, lo, hi, opens, width):
             rows = slice(g * P, (g + 1) * P)
             steps = [
                 (weights, moving, at)
                 for weights, moving in ((w_ctx_sb, ctx_sb), (w_hh_sb, h0_sb))
-                for at in range(lo, hi, PLAIN)
+                for at in range(lo, hi, width)
             ]
             for step, (weights, moving, at) in enumerate(steps):
                 nc.tensor.matmul(
-                    pre[g, lo][:, at - lo : at - lo + PLAIN],
+                    pre[g, lo][:, at - lo : at - lo + width],
                     weights[:, rows],
-                    columns(moving, at, at + PLAIN),
+                    columns(moving, at, at + width),
                     start=opens and step == 0,
                     stop=not opens and step == len(steps) - 1,
                 )
@@ -121,7 +121,7 @@ def tile_pgndecoder_kernel(tc, table, w_emb, ctx, w_ctx, h0, w_hh, b, c0, offs, 
             nc.tensor.matmul(pre[GATE_OUT, PIECE][:, 0:P], zeros[:], zeros[:], start=True, stop=True)
 
         for g in CELL_GATES + (GATE_OUT,):
-            plain_products(g, *FIRST, opens=True)
+            plain_products(g, *FIRST, opens=True, width=PIECE)
         for g in CELL_GATES:
             looked_up_product(g, *FIRST, opens=False)
         for g in CELL_GATES:
@@ -130,7 +130,7 @@ def tile_pgndecoder_kernel(tc, table, w_emb, ctx, w_ctx, h0, w_hh, b, c0, offs, 
         tanh_of_cell(*FIRST)
 
         for g in CELL_GATES:
-            plain_products(g, *SECOND, opens=False)
+            plain_products(g, *SECOND, opens=False, width=NARROW)
         new_cell_state(SECOND)
 
         last_lo, last_hi = SECOND_HALVES[1]
@@ -139,7 +139,7 @@ def tile_pgndecoder_kernel(tc, table, w_emb, ctx, w_ctx, h0, w_hh, b, c0, offs, 
         for half in SECOND_HALVES:
             looked_up_product(GATE_OUT, *half, opens=True)
         for half in SECOND_HALVES:
-            plain_products(GATE_OUT, *half, opens=False)
+            plain_products(GATE_OUT, *half, opens=False, width=PIECE // 2)
 
         new_hidden_state(squash(GATE_OUT, *FIRST), *FIRST)
         for half in SECOND_HALVES:

@@ -48,7 +48,8 @@ def tile_pgndecoder_kernel(tc, table, w_emb, ctx, w_ctx, h0, w_hh, b, c0, offs, 
         nc.scalar.dma_start(h0_sb[0][:], h0[:, 0:PIECE])
         nc.sync.dma_start(offsets[:], offs)
         nc.scalar.dma_start(w_emb_sb[:], w_emb)
-        nc.sync.dma_start(table_sb[:], table)
+        nc.sync.dma_start(table_sb[:, 0 : V // 2], table[:, 0 : V // 2])
+        nc.scalar.dma_start(table_sb[:, V // 2 : V], table[:, V // 2 : V])
         with nc.allow_non_contiguous_dma(reason="512 bias values, one to a partition and gate"):
             nc.scalar.dma_start(bias_sb[:], b.rearrange("(g p) o -> p (g o)", p=P))
         nc.sync.dma_start(c0_sb[0][:], c0[:, 0:PIECE])

@@ -11,10 +11,20 @@ PIECE = 512
 NARROW = 128
 GATE_IN, GATE_FORGET, GATE_CANDIDATE, GATE_OUT = 0, 1, 2, 3
 GATES = 4
-CELL_GATES = (GATE_IN, GATE_CANDIDATE, GATE_FORGET)
-FIRST, SECOND = (0, PIECE), (PIECE, N)
-SECOND_HALVES = ((PIECE, PIECE + PIECE // 2), (PIECE + PIECE // 2, N))
-CUTS = {FIRST: (FIRST,), SECOND: SECOND_HALVES}
+FIRST = (0, PIECE)
+SECOND = (PIECE, PIECE + PIECE // 2)
+THIRD = (PIECE + PIECE // 2, N)
+PIECES = (FIRST, SECOND, THIRD)
+CELL_GATES = {
+    FIRST: (GATE_IN, GATE_CANDIDATE, GATE_FORGET),
+    SECOND: (GATE_IN, GATE_CANDIDATE, GATE_FORGET),
+    THIRD: (GATE_FORGET, GATE_IN, GATE_CANDIDATE),
+}
+PARTS = {
+    FIRST: ((0, PIECE // 2), (PIECE // 2, PIECE)),
+    SECOND: (SECOND,),
+    THIRD: ((THIRD[0], THIRD[0] + PIECE // 4), (THIRD[0] + PIECE // 4, N)),
+}
 WARM_UP_MATMULS = 16
 
 FLOPS = 2 * 3 * P * GATES * P * N
@@ -28,38 +38,55 @@ def tile_pgndecoder_kernel(tc, table, w_emb, ctx, w_ctx, h0, w_hh, b, c0, offs, 
     ):
         offsets = held.tile([P, N // 16], U16, name="offsets")
         table_sb = held.tile([P, V], BF16, name="table_sb")
-        w_emb_sb = held.tile([P, GATES * P], BF16, name="w_emb_sb")
+        w_emb_cell_sb = held.tile([P, GATE_OUT * P], BF16, name="w_emb_cell_sb")
+        w_emb_out_sb = held.tile([P, P], BF16, name="w_emb_out_sb")
         w_ctx_sb = held.tile([P, GATES * P], BF16, name="w_ctx_sb")
         w_hh_sb = held.tile([P, GATES * P], BF16, name="w_hh_sb")
-        ctx_sb = [held.tile([P, PIECE], BF16, name=f"ctx_sb{lo}") for lo, hi in (FIRST, SECOND)]
-        h0_sb = [held.tile([P, PIECE], BF16, name=f"h0_sb{lo}") for lo, hi in (FIRST, SECOND)]
-        c0_sb = [held.tile([P, PIECE], F32, name=f"c0_sb{lo}") for lo, hi in (FIRST, SECOND)]
+        ctx_sb = {(lo, hi): held.tile([P, hi - lo], BF16, name=f"ctx_sb{lo}") for lo, hi in PIECES}
+        h0_sb = {(lo, hi): held.tile([P, hi - lo], BF16, name=f"h0_sb{lo}") for lo, hi in PIECES}
+        c0_sb = {(lo, hi): held.tile([P, hi - lo], F32, name=f"c0_sb{lo}") for lo, hi in PIECES}
         bias_sb = held.tile([P, GATES], F32, name="bias_sb")
 
-        def columns(piece_tiles, lo, hi):
-            return piece_tiles[lo // PIECE][:, lo % PIECE : lo % PIECE + hi - lo]
+        def columns(tiles, piece, lo, hi):
+            return tiles[piece][:, lo - piece[0] : hi - piece[0]]
 
         zeros = held.tile([P, P], BF16, name="zeros")
         nc.gpsimd.memset(zeros[:], 0.0)
+        with nc.allow_non_contiguous_dma(reason="512 bias values, one to a partition and gate"):
+            nc.gpsimd.dma_start(bias_sb[:], b.rearrange("(g p) o -> p (g o)", p=P))
 
         nc.sync.dma_start(w_ctx_sb[:], w_ctx)
-        nc.scalar.dma_start(ctx_sb[0][:], ctx[:, 0:PIECE])
+        nc.scalar.dma_start(ctx_sb[FIRST][:], ctx[:, 0:PIECE])
         nc.sync.dma_start(w_hh_sb[:], w_hh)
-        nc.scalar.dma_start(h0_sb[0][:], h0[:, 0:PIECE])
+        nc.scalar.dma_start(h0_sb[FIRST][:], h0[:, 0:PIECE])
         nc.sync.dma_start(offsets[:], offs)
-        nc.scalar.dma_start(w_emb_sb[:], w_emb)
+        nc.scalar.dma_start(w_emb_cell_sb[:], w_emb[:, 0 : GATE_OUT * P])
         nc.sync.dma_start(table_sb[:, 0 : V // 2], table[:, 0 : V // 2])
         nc.scalar.dma_start(table_sb[:, V // 2 : V], table[:, V // 2 : V])
-        with nc.allow_non_contiguous_dma(reason="512 bias values, one to a partition and gate"):
-            nc.scalar.dma_start(bias_sb[:], b.rearrange("(g p) o -> p (g o)", p=P))
-        nc.sync.dma_start(c0_sb[0][:], c0[:, 0:PIECE])
-        nc.sync.dma_start(ctx_sb[1][:], ctx[:, PIECE:N])
-        nc.sync.dma_start(h0_sb[1][:], h0[:, PIECE:N])
-        nc.sync.dma_start(c0_sb[1][:], c0[:, PIECE:N])
 
-        pre = {(g, lo): psum.tile([P, hi - lo], F32, name=f"pre{g}_{lo}") for g in CELL_GATES for lo, hi in (FIRST, SECOND)}
-        pre[GATE_OUT, 0] = psum.tile([P, PIECE], F32, name=f"pre{GATE_OUT}_0")
-        pre[GATE_OUT, PIECE] = psum.tile([P, PIECE // 2], F32, name=f"pre{GATE_OUT}_{PIECE}")
+        squashed_zero = held.tile([P, 1], F32, name="squashed_zero")
+        nc.scalar.activation(squashed_zero[:], zeros[:, 0:1], SIGMOID)
+
+        nc.sync.dma_start(c0_sb[FIRST][:], c0[:, 0:PIECE])
+        for lo, hi in (SECOND, THIRD):
+            nc.sync.dma_start(ctx_sb[lo, hi][:], ctx[:, lo:hi])
+            nc.sync.dma_start(h0_sb[lo, hi][:], h0[:, lo:hi])
+            nc.sync.dma_start(c0_sb[lo, hi][:], c0[:, lo:hi])
+        nc.sync.dma_start(w_emb_out_sb[:], w_emb[:, GATE_OUT * P : GATES * P])
+
+        pre = {}
+
+        def open_bank(g, piece, successor_of=None):
+            lo, hi = piece
+            name = f"pre{g}_{lo}"
+            tag = name if successor_of is None else f"pre{successor_of[0]}_{successor_of[1][0]}"
+            pre[g, lo] = psum.tile([P, hi - lo], F32, name=name, tag=tag)
+
+        for g in range(GATES):
+            open_bank(g, FIRST)
+        for g in CELL_GATES[SECOND]:
+            open_bank(g, SECOND)
+        open_bank(CELL_GATES[THIRD][0], THIRD)
 
         def plain_products(g, lo, hi, opens, width):
             rows = slice(g * P, (g + 1) * P)
@@ -72,78 +99,114 @@ def tile_pgndecoder_kernel(tc, table, w_emb, ctx, w_ctx, h0, w_hh, b, c0, offs, 
                 nc.tensor.matmul(
                     pre[g, lo][:, at - lo : at - lo + width],
                     weights[:, rows],
-                    columns(moving, at, at + width),
+                    columns(moving, (lo, hi), at, at + width),
                     start=opens and step == 0,
                     stop=not opens and step == len(steps) - 1,
                 )
 
         def looked_up_product(g, lo, hi, opens):
-            rows = slice(g * P, (g + 1) * P)
+            weights = w_emb_out_sb[:] if g == GATE_OUT else w_emb_cell_sb[:, g * P : (g + 1) * P]
             nc.tensor.matmul(
                 pre[g, lo][:],
-                w_emb_sb[:, rows],
+                weights,
                 table_sb[:].indirect(offsets[:, lo // 16 : hi // 16]),
                 start=opens,
                 stop=not opens,
             )
 
-        def squash(g, lo, hi):
-            squashed = held.tile([P, hi - lo], F32, name=f"gate{g}_{lo}")
-            nc.scalar.activation(
-                squashed[:], pre[g, lo][:], TANH if g == GATE_CANDIDATE else SIGMOID, bias=bias_sb[:, g : g + 1]
-            )
+        def squash(g, piece, stretches):
+            start = piece[0]
+            squashed = {}
+            for lo, hi in stretches:
+                gate = held.tile([P, hi - lo], F32, name=f"gate{g}_{lo}")
+                nc.scalar.activation(
+                    gate[:],
+                    pre[g, start][:, lo - start : hi - start],
+                    TANH if g == GATE_CANDIDATE else SIGMOID,
+                    bias=bias_sb[:, g : g + 1],
+                )
+                for part in PARTS[piece]:
+                    if lo <= part[0] and part[1] <= hi:
+                        squashed[part] = gate[:, part[0] - lo : part[1] - lo]
             return squashed
 
         cell = {}
         tanh_cell = {}
 
         def new_cell_state(piece):
-            start = piece[0]
-            gate_in, gate_candidate, gate_forget = [squash(g, *piece) for g in CELL_GATES]
-            for lo, hi in CUTS[piece]:
-                cut = slice(lo - start, hi - start)
-                fresh = held.tile([P, hi - lo], F32, name=f"fresh{lo}")
-                nc.vector.tensor_tensor(fresh[:], gate_in[:, cut], gate_candidate[:, cut], MULT)
-                kept = held.tile([P, hi - lo], F32, name=f"kept{lo}")
-                nc.vector.tensor_tensor(kept[:], gate_forget[:, cut], columns(c0_sb, lo, hi), MULT)
-                cell[lo] = held.tile([P, hi - lo], F32, name=f"cell{lo}")
-                nc.vector.tensor_tensor(cell[lo][:], kept[:], fresh[:], ADD)
+            squashed = {}
+            for g in CELL_GATES[piece]:
+                by_part = piece == THIRD and g == CELL_GATES[piece][-1]
+                squashed[g] = squash(g, piece, PARTS[piece] if by_part else (piece,))
+            fresh = {}
+            kept = {}
 
-        def tanh_of_cell(lo, hi):
-            tanh_cell[lo] = held.tile([P, hi - lo], F32, name=f"tanh_cell{lo}")
-            nc.scalar.activation(tanh_cell[lo][:], cell[lo][:], TANH)
+            def multiply_input_and_candidate():
+                for lo, hi in PARTS[piece]:
+                    fresh[lo] = held.tile([P, hi - lo], F32, name=f"fresh{lo}")
+                    nc.vector.tensor_tensor(fresh[lo][:], squashed[GATE_IN][lo, hi], squashed[GATE_CANDIDATE][lo, hi], MULT)
 
-        def new_hidden_state(gate_out, lo, hi):
-            hidden = held.tile([P, hi - lo], F32, name=f"hidden{lo}")
-            nc.vector.tensor_tensor(hidden[:], gate_out[:], tanh_cell[lo][:], MULT)
-            nc.sync.dma_start(out[:, lo:hi], hidden[:])
+            def multiply_forget_and_old_state():
+                for lo, hi in PARTS[piece]:
+                    kept[lo] = held.tile([P, hi - lo], F32, name=f"kept{lo}")
+                    nc.vector.tensor_tensor(kept[lo][:], squashed[GATE_FORGET][lo, hi], columns(c0_sb, piece, lo, hi), MULT)
+
+            if CELL_GATES[piece][0] == GATE_FORGET:
+                multiply_forget_and_old_state()
+                multiply_input_and_candidate()
+            else:
+                multiply_input_and_candidate()
+                multiply_forget_and_old_state()
+            for lo, hi in PARTS[piece]:
+                cell[lo, hi] = held.tile([P, hi - lo], F32, name=f"cell{lo}")
+                nc.vector.tensor_tensor(cell[lo, hi][:], kept[lo][:], fresh[lo][:], ADD)
+
+        def tanh_of_cell(piece):
+            for part in PARTS[piece]:
+                lo, hi = part
+                tanh_cell[part] = held.tile([P, hi - lo], F32, name=f"tanh_cell{lo}")
+                nc.scalar.activation(tanh_cell[part][:], cell[part][:], TANH)
+
+        def new_hidden_state(gate_out, piece):
+            for part in PARTS[piece]:
+                lo, hi = part
+                hidden = held.tile([P, hi - lo], F32, name=f"hidden{lo}")
+                nc.vector.tensor_tensor(hidden[:], gate_out[part], tanh_cell[part][:], MULT)
+                nc.sync.dma_start(out[:, lo:hi], hidden[:])
 
         for repeat in range(WARM_UP_MATMULS):
-            nc.tensor.matmul(pre[GATE_OUT, PIECE][:, 0:P], zeros[:], zeros[:], start=True, stop=True)
+            nc.tensor.matmul(pre[CELL_GATES[THIRD][0], THIRD[0]][:, 0:P], zeros[:], zeros[:], start=True, stop=True)
 
-        for g in CELL_GATES + (GATE_OUT,):
+        for g in CELL_GATES[FIRST] + (GATE_OUT,):
             plain_products(g, *FIRST, opens=True, width=PIECE)
-        for g in CELL_GATES:
+        for g in CELL_GATES[FIRST]:
             looked_up_product(g, *FIRST, opens=False)
-        for g in CELL_GATES:
+        for g in CELL_GATES[SECOND]:
             looked_up_product(g, *SECOND, opens=True)
         new_cell_state(FIRST)
-        tanh_of_cell(*FIRST)
+        tanh_of_cell(FIRST)
 
-        for g in CELL_GATES:
+        for g in CELL_GATES[SECOND]:
             plain_products(g, *SECOND, opens=False, width=NARROW)
         new_cell_state(SECOND)
 
-        last_lo, last_hi = SECOND_HALVES[1]
-        pre[GATE_OUT, last_lo] = psum.tile([P, last_hi - last_lo], F32, name=f"pre{GATE_OUT}_{last_lo}", tag=f"pre{GATE_IN}_0")
-        looked_up_product(GATE_OUT, *FIRST, opens=False)
-        for half in SECOND_HALVES:
-            looked_up_product(GATE_OUT, *half, opens=True)
-        for half in SECOND_HALVES:
-            plain_products(GATE_OUT, *half, opens=False, width=PIECE // 2)
+        open_bank(CELL_GATES[THIRD][1], THIRD, successor_of=(CELL_GATES[FIRST][0], FIRST))
+        open_bank(CELL_GATES[THIRD][2], THIRD, successor_of=(CELL_GATES[FIRST][1], FIRST))
+        for g in CELL_GATES[THIRD]:
+            plain_products(g, *THIRD, opens=True, width=NARROW)
+        for g in CELL_GATES[THIRD]:
+            looked_up_product(g, *THIRD, opens=False)
+        new_cell_state(THIRD)
 
-        new_hidden_state(squash(GATE_OUT, *FIRST), *FIRST)
-        for half in SECOND_HALVES:
-            tanh_of_cell(*half)
-        for half in SECOND_HALVES:
-            new_hidden_state(squash(GATE_OUT, *half), *half)
+        open_bank(GATE_OUT, SECOND, successor_of=(CELL_GATES[FIRST][2], FIRST))
+        open_bank(GATE_OUT, THIRD, successor_of=(CELL_GATES[SECOND][0], SECOND))
+        looked_up_product(GATE_OUT, *FIRST, opens=False)
+        for piece in (SECOND, THIRD):
+            looked_up_product(GATE_OUT, *piece, opens=True)
+        for piece in (SECOND, THIRD):
+            plain_products(GATE_OUT, *piece, opens=False, width=PIECE // 2)
+        tanh_of_cell(SECOND)
+        new_hidden_state(squash(GATE_OUT, FIRST, (FIRST,)), FIRST)
+        tanh_of_cell(THIRD)
+        new_hidden_state(squash(GATE_OUT, SECOND, (SECOND,)), SECOND)
+        new_hidden_state(squash(GATE_OUT, THIRD, PARTS[THIRD]), THIRD)

@@ -52,8 +52,6 @@ def tile_pgndecoder_kernel(tc, table, w_emb, ctx, w_ctx, h0, w_hh, b, c0, offs, 
 
         zeros = held.tile([P, P], BF16, name="zeros")
         nc.gpsimd.memset(zeros[:], 0.0)
-        with nc.allow_non_contiguous_dma(reason="512 bias values, one to a partition and gate"):
-            nc.gpsimd.dma_start(bias_sb[:], b.rearrange("(g p) o -> p (g o)", p=P))
 
         nc.sync.dma_start(w_ctx_sb[:], w_ctx)
         nc.scalar.dma_start(ctx_sb[FIRST][:], ctx[:, 0:PIECE])
@@ -66,6 +64,9 @@ def tile_pgndecoder_kernel(tc, table, w_emb, ctx, w_ctx, h0, w_hh, b, c0, offs, 
 
         squashed_zero = held.tile([P, 1], F32, name="squashed_zero")
         nc.scalar.activation(squashed_zero[:], zeros[:, 0:1], SIGMOID)
+
+        with nc.allow_non_contiguous_dma(reason="512 bias values, one to a partition and gate"):
+            nc.scalar.dma_start(bias_sb[:], b.rearrange("(g p) o -> p (g o)", p=P))
 
         nc.sync.dma_start(c0_sb[FIRST][:], c0[:, 0:PIECE])
         for lo, hi in (SECOND, THIRD):

@@ -115,7 +115,7 @@ def tile_pgndecoder_kernel(tc, table, w_emb, ctx, w_ctx, h0, w_hh, b, c0, offs, 
                 stop=not opens,
             )
 
-        def squash(g, piece, stretches):
+        def squash(g, piece, stretches, bias):
             start = piece[0]
             squashed = {}
             for lo, hi in stretches:
@@ -124,7 +124,7 @@ def tile_pgndecoder_kernel(tc, table, w_emb, ctx, w_ctx, h0, w_hh, b, c0, offs, 
                     gate[:],
                     pre[g, start][:, lo - start : hi - start],
                     TANH if g == GATE_CANDIDATE else SIGMOID,
-                    bias=bias_sb[:, g : g + 1],
+                    bias=bias[:, g : g + 1],
                 )
                 for part in PARTS[piece]:
                     if lo <= part[0] and part[1] <= hi:
@@ -134,11 +134,11 @@ def tile_pgndecoder_kernel(tc, table, w_emb, ctx, w_ctx, h0, w_hh, b, c0, offs, 
         cell = {}
         tanh_cell = {}
 
-        def new_cell_state(piece):
+        def new_cell_state(piece, bias):
             squashed = {}
             for g in CELL_GATES[piece]:
                 by_part = piece == THIRD and g == CELL_GATES[piece][-1]
-                squashed[g] = squash(g, piece, PARTS[piece] if by_part else (piece,))
+                squashed[g] = squash(g, piece, PARTS[piece] if by_part else (piece,), bias)
             fresh = {}
             kept = {}
 
@@ -162,6 +162,11 @@ def tile_pgndecoder_kernel(tc, table, w_emb, ctx, w_ctx, h0, w_hh, b, c0, offs, 
                 cell[lo, hi] = held.tile([P, hi - lo], F32, name=f"cell{lo}")
                 nc.vector.tensor_tensor(cell[lo, hi][:], kept[lo][:], fresh[lo][:], ADD)
 
+        def copy_bias_behind_cell_state(piece):
+            copied = held.tile([P, GATES], F32, name=f"bias_behind{piece[0]}", tag=f"kept{PARTS[piece][-1][0]}")
+            nc.vector.tensor_copy(copied[:], bias_sb[:])
+            return copied
+
         def tanh_of_cell(piece):
             for part in PARTS[piece]:
                 lo, hi = part
@@ -184,12 +189,14 @@ def tile_pgndecoder_kernel(tc, table, w_emb, ctx, w_ctx, h0, w_hh, b, c0, offs, 
             looked_up_product(g, *FIRST, opens=False)
         for g in CELL_GATES[SECOND]:
             looked_up_product(g, *SECOND, opens=True)
-        new_cell_state(FIRST)
+        new_cell_state(FIRST, bias_sb)
+        bias_behind_first = copy_bias_behind_cell_state(FIRST)
         tanh_of_cell(FIRST)
 
         for g in CELL_GATES[SECOND]:
             plain_products(g, *SECOND, opens=False, width=NARROW)
-        new_cell_state(SECOND)
+        new_cell_state(SECOND, bias_sb)
+        bias_behind_second = copy_bias_behind_cell_state(SECOND)
 
         open_bank(CELL_GATES[THIRD][1], THIRD, successor_of=(CELL_GATES[FIRST][0], FIRST))
         open_bank(CELL_GATES[THIRD][2], THIRD, successor_of=(CELL_GATES[FIRST][1], FIRST))
@@ -197,7 +204,7 @@ def tile_pgndecoder_kernel(tc, table, w_emb, ctx, w_ctx, h0, w_hh, b, c0, offs, 
             plain_products(g, *THIRD, opens=True, width=NARROW)
         for g in CELL_GATES[THIRD]:
             looked_up_product(g, *THIRD, opens=False)
-        new_cell_state(THIRD)
+        new_cell_state(THIRD, bias_behind_first)
 
         open_bank(GATE_OUT, SECOND, successor_of=(CELL_GATES[FIRST][2], FIRST))
         open_bank(GATE_OUT, THIRD, successor_of=(CELL_GATES[SECOND][0], SECOND))
@@ -207,7 +214,7 @@ def tile_pgndecoder_kernel(tc, table, w_emb, ctx, w_ctx, h0, w_hh, b, c0, offs, 
         for piece in (SECOND, THIRD):
             plain_products(GATE_OUT, *piece, opens=False, width=PIECE // 2)
         tanh_of_cell(SECOND)
-        new_hidden_state(squash(GATE_OUT, FIRST, (FIRST,)), FIRST)
+        new_hidden_state(squash(GATE_OUT, FIRST, (FIRST,), bias_behind_second), FIRST)
         tanh_of_cell(THIRD)
-        new_hidden_state(squash(GATE_OUT, SECOND, (SECOND,)), SECOND)
-        new_hidden_state(squash(GATE_OUT, THIRD, PARTS[THIRD]), THIRD)
+        new_hidden_state(squash(GATE_OUT, SECOND, (SECOND,), bias_behind_second), SECOND)
+        new_hidden_state(squash(GATE_OUT, THIRD, PARTS[THIRD], bias_behind_second), THIRD)

@@ -115,21 +115,12 @@ def tile_pgndecoder_kernel(tc, table, w_emb, ctx, w_ctx, h0, w_hh, b, c0, offs, 
                 stop=not opens,
             )
 
-        def squash(g, piece, stretches, bias):
-            start = piece[0]
-            squashed = {}
-            for lo, hi in stretches:
-                gate = held.tile([P, hi - lo], F32, name=f"gate{g}_{lo}")
-                nc.scalar.activation(
-                    gate[:],
-                    pre[g, start][:, lo - start : hi - start],
-                    TANH if g == GATE_CANDIDATE else SIGMOID,
-                    bias=bias[:, g : g + 1],
-                )
-                for part in PARTS[piece]:
-                    if lo <= part[0] and part[1] <= hi:
-                        squashed[part] = gate[:, part[0] - lo : part[1] - lo]
-            return squashed
+        def squash(g, piece, bias):
+            start, end = piece
+            gate = held.tile([P, end - start], F32, name=f"gate{g}_{start}")
+            function = TANH if g == GATE_CANDIDATE else SIGMOID
+            nc.scalar.activation(gate[:], pre[g, start][:], function, bias=bias[:, g : g + 1])
+            return {(lo, hi): gate[:, lo - start : hi - start] for lo, hi in PARTS[piece]}
 
         cell = {}
         tanh_cell = {}
@@ -137,8 +128,7 @@ def tile_pgndecoder_kernel(tc, table, w_emb, ctx, w_ctx, h0, w_hh, b, c0, offs, 
         def new_cell_state(piece, bias):
             squashed = {}
             for g in CELL_GATES[piece]:
-                by_part = piece == THIRD and g == CELL_GATES[piece][-1]
-                squashed[g] = squash(g, piece, PARTS[piece] if by_part else (piece,), bias)
+                squashed[g] = squash(g, piece, bias)
             fresh = {}
             kept = {}
 
@@ -158,9 +148,10 @@ def tile_pgndecoder_kernel(tc, table, w_emb, ctx, w_ctx, h0, w_hh, b, c0, offs, 
             else:
                 multiply_input_and_candidate()
                 multiply_forget_and_old_state()
+            start, end = piece
+            cell[piece] = held.tile([P, end - start], F32, name=f"cell{start}")
             for lo, hi in PARTS[piece]:
-                cell[lo, hi] = held.tile([P, hi - lo], F32, name=f"cell{lo}")
-                nc.vector.tensor_tensor(cell[lo, hi][:], kept[lo][:], fresh[lo][:], ADD)
+                nc.vector.tensor_tensor(cell[piece][:, lo - start : hi - start], kept[lo][:], fresh[lo][:], ADD)
 
         def copy_bias_behind_cell_state(piece):
             copied = held.tile([P, GATES], F32, name=f"bias_behind{piece[0]}", tag=f"kept{PARTS[piece][-1][0]}")
@@ -168,16 +159,17 @@ def tile_pgndecoder_kernel(tc, table, w_emb, ctx, w_ctx, h0, w_hh, b, c0, offs, 
             return copied
 
         def tanh_of_cell(piece):
-            for part in PARTS[piece]:
-                lo, hi = part
-                tanh_cell[part] = held.tile([P, hi - lo], F32, name=f"tanh_cell{lo}")
-                nc.scalar.activation(tanh_cell[part][:], cell[part][:], TANH)
+            start, end = piece
+            tanh_cell[piece] = held.tile([P, end - start], F32, name=f"tanh_cell{start}")
+            for lo, hi in PARTS[piece] if piece == THIRD else (piece,):
+                columns_of_part = slice(lo - start, hi - start)
+                nc.scalar.activation(tanh_cell[piece][:, columns_of_part], cell[piece][:, columns_of_part], TANH)
 
         def new_hidden_state(gate_out, piece):
-            for part in PARTS[piece]:
-                lo, hi = part
+            start = piece[0]
+            for lo, hi in PARTS[piece]:
                 hidden = held.tile([P, hi - lo], F32, name=f"hidden{lo}")
-                nc.vector.tensor_tensor(hidden[:], gate_out[part], tanh_cell[part][:], MULT)
+                nc.vector.tensor_tensor(hidden[:], gate_out[lo, hi], tanh_cell[piece][:, lo - start : hi - start], MULT)
                 nc.sync.dma_start(out[:, lo:hi], hidden[:])
 
         for repeat in range(WARM_UP_MATMULS):
@@ -214,7 +206,7 @@ def tile_pgndecoder_kernel(tc, table, w_emb, ctx, w_ctx, h0, w_hh, b, c0, offs, 
         for piece in (SECOND, THIRD):
             plain_products(GATE_OUT, *piece, opens=False, width=PIECE // 2)
         tanh_of_cell(SECOND)
-        new_hidden_state(squash(GATE_OUT, FIRST, (FIRST,), bias_behind_second), FIRST)
+        new_hidden_state(squash(GATE_OUT, FIRST, bias_behind_second), FIRST)
         tanh_of_cell(THIRD)
-        new_hidden_state(squash(GATE_OUT, SECOND, (SECOND,), bias_behind_second), SECOND)
-        new_hidden_state(squash(GATE_OUT, THIRD, PARTS[THIRD], bias_behind_second), THIRD)
+        new_hidden_state(squash(GATE_OUT, SECOND, bias_behind_second), SECOND)
+        new_hidden_state(squash(GATE_OUT, THIRD, bias_behind_second), THIRD)

@@ -25,7 +25,7 @@ PARTS = {
     SECOND: (SECOND,),
     THIRD: ((THIRD[0], THIRD[0] + PIECE // 4), (THIRD[0] + PIECE // 4, N)),
 }
-WARM_UP_MATMULS = 16
+WARM_UP_MATMULS = 14
 
 FLOPS = 2 * 3 * P * GATES * P * N
 
@@ -51,20 +51,21 @@ def tile_pgndecoder_kernel(tc, table, w_emb, ctx, w_ctx, h0, w_hh, b, c0, offs, 
             return tiles[piece][:, lo - piece[0] : hi - piece[0]]
 
         zeros = held.tile([P, P], BF16, name="zeros")
-        nc.gpsimd.memset(zeros[:], 0.0)
+        nc.vector.memset(zeros[:], 0.0)
 
         nc.sync.dma_start(w_ctx_sb[:], w_ctx)
         nc.scalar.dma_start(ctx_sb[FIRST][:], ctx[:, 0:PIECE])
         nc.sync.dma_start(w_hh_sb[:], w_hh)
         nc.scalar.dma_start(h0_sb[FIRST][:], h0[:, 0:PIECE])
         nc.sync.dma_start(offsets[:], offs)
-        nc.scalar.dma_start(w_emb_cell_sb[:], w_emb[:, 0 : GATE_OUT * P])
+        nc.scalar.dma_start(w_emb_cell_sb[:, 0:P], w_emb[:, 0:P])
         nc.sync.dma_start(table_sb[:, 0 : V // 2], table[:, 0 : V // 2])
         nc.scalar.dma_start(table_sb[:, V // 2 : V], table[:, V // 2 : V])
 
         squashed_zero = held.tile([P, 1], F32, name="squashed_zero")
         nc.scalar.activation(squashed_zero[:], zeros[:, 0:1], SIGMOID)
 
+        nc.sync.dma_start(w_emb_cell_sb[:, P : GATE_OUT * P], w_emb[:, P : GATE_OUT * P])
         with nc.allow_non_contiguous_dma(reason="512 bias values, one to a partition and gate"):
             nc.scalar.dma_start(bias_sb[:], b.rearrange("(g p) o -> p (g o)", p=P))
 

import concourse.mybir as mybir

BF16, F32, U16 = mybir.dt.bfloat16, mybir.dt.float32, mybir.dt.uint16
SIGMOID, TANH = mybir.ActivationFunctionType.Sigmoid, mybir.ActivationFunctionType.Tanh
MULT, ADD = mybir.AluOpType.mult, mybir.AluOpType.add

P = 128
V = 2048
N = 1024
PIECE = 512
NARROW = 128
GATE_IN, GATE_FORGET, GATE_CANDIDATE, GATE_OUT = 0, 1, 2, 3
GATES = 4
FIRST = (0, PIECE)
SECOND = (PIECE, PIECE + PIECE // 2)
THIRD = (PIECE + PIECE // 2, N)
PIECES = (FIRST, SECOND, THIRD)
CELL_GATES = {
    FIRST: (GATE_IN, GATE_CANDIDATE, GATE_FORGET),
    SECOND: (GATE_IN, GATE_CANDIDATE, GATE_FORGET),
    THIRD: (GATE_FORGET, GATE_IN, GATE_CANDIDATE),
}
PARTS = {
    FIRST: ((0, PIECE // 2), (PIECE // 2, PIECE)),
    SECOND: (SECOND,),
    THIRD: ((THIRD[0], THIRD[0] + PIECE // 4), (THIRD[0] + PIECE // 4, N)),
}
WARM_UP_MATMULS = 14

FLOPS = 2 * 3 * P * GATES * P * N


def tile_pgndecoder_kernel(tc, table, w_emb, ctx, w_ctx, h0, w_hh, b, c0, offs, out):
    nc = tc.nc
    with (
        tc.tile_pool(name="held", bufs=1) as held,
        tc.psum_pool(name="psum", bufs=1) as psum,
    ):
        offsets = held.tile([P, N // 16], U16, name="offsets")
        table_sb = held.tile([P, V], BF16, name="table_sb")
        w_emb_cell_sb = held.tile([P, GATE_OUT * P], BF16, name="w_emb_cell_sb")
        w_emb_out_sb = held.tile([P, P], BF16, name="w_emb_out_sb")
        w_ctx_sb = held.tile([P, GATES * P], BF16, name="w_ctx_sb")
        w_hh_sb = held.tile([P, GATES * P], BF16, name="w_hh_sb")
        ctx_sb = {(lo, hi): held.tile([P, hi - lo], BF16, name=f"ctx_sb{lo}") for lo, hi in PIECES}
        h0_sb = {(lo, hi): held.tile([P, hi - lo], BF16, name=f"h0_sb{lo}") for lo, hi in PIECES}
        c0_sb = {(lo, hi): held.tile([P, hi - lo], F32, name=f"c0_sb{lo}") for lo, hi in PIECES}
        bias_sb = held.tile([P, GATES], F32, name="bias_sb")

        def columns(tiles, piece, lo, hi):
            return tiles[piece][:, lo - piece[0] : hi - piece[0]]

        zeros = held.tile([P, P], BF16, name="zeros")
        nc.vector.memset(zeros[:], 0.0)

        nc.sync.dma_start(w_ctx_sb[:], w_ctx)
        nc.scalar.dma_start(ctx_sb[FIRST][:], ctx[:, 0:PIECE])
        nc.sync.dma_start(w_hh_sb[:], w_hh)
        nc.scalar.dma_start(h0_sb[FIRST][:], h0[:, 0:PIECE])
        nc.sync.dma_start(offsets[:], offs)
        nc.scalar.dma_start(w_emb_cell_sb[:, 0:P], w_emb[:, 0:P])
        nc.sync.dma_start(table_sb[:, 0 : V // 2], table[:, 0 : V // 2])
        nc.scalar.dma_start(table_sb[:, V // 2 : V], table[:, V // 2 : V])

        squashed_zero = held.tile([P, 1], F32, name="squashed_zero")
        nc.scalar.activation(squashed_zero[:], zeros[:, 0:1], SIGMOID)

        nc.sync.dma_start(w_emb_cell_sb[:, P : GATE_OUT * P], w_emb[:, P : GATE_OUT * P])
        with nc.allow_non_contiguous_dma(reason="512 bias values, one to a partition and gate"):
            nc.scalar.dma_start(bias_sb[:], b.rearrange("(g p) o -> p (g o)", p=P))

        nc.sync.dma_start(c0_sb[FIRST][:], c0[:, 0:PIECE])
        for lo, hi in (SECOND, THIRD):
            nc.sync.dma_start(ctx_sb[lo, hi][:], ctx[:, lo:hi])
            nc.sync.dma_start(h0_sb[lo, hi][:], h0[:, lo:hi])
            nc.sync.dma_start(c0_sb[lo, hi][:], c0[:, lo:hi])
        nc.sync.dma_start(w_emb_out_sb[:], w_emb[:, GATE_OUT * P : GATES * P])

        pre = {}

        def open_bank(g, piece, successor_of=None):
            lo, hi = piece
            name = f"pre{g}_{lo}"
            tag = name if successor_of is None else f"pre{successor_of[0]}_{successor_of[1][0]}"
            pre[g, lo] = psum.tile([P, hi - lo], F32, name=name, tag=tag)

        for g in range(GATES):
            open_bank(g, FIRST)
        for g in CELL_GATES[SECOND]:
            open_bank(g, SECOND)
        open_bank(CELL_GATES[THIRD][0], THIRD)

        def plain_products(g, lo, hi, opens, width):
            rows = slice(g * P, (g + 1) * P)
            steps = [
                (weights, moving, at)
                for weights, moving in ((w_ctx_sb, ctx_sb), (w_hh_sb, h0_sb))
                for at in range(lo, hi, width)
            ]
            for step, (weights, moving, at) in enumerate(steps):
                nc.tensor.matmul(
                    pre[g, lo][:, at - lo : at - lo + width],
                    weights[:, rows],
                    columns(moving, (lo, hi), at, at + width),
                    start=opens and step == 0,
                    stop=not opens and step == len(steps) - 1,
                )

        def looked_up_product(g, lo, hi, opens):
            weights = w_emb_out_sb[:] if g == GATE_OUT else w_emb_cell_sb[:, g * P : (g + 1) * P]
            nc.tensor.matmul(
                pre[g, lo][:],
                weights,
                table_sb[:].indirect(offsets[:, lo // 16 : hi // 16]),
                start=opens,
                stop=not opens,
            )

        def squash(g, piece, bias):
            start, end = piece
            gate = held.tile([P, end - start], F32, name=f"gate{g}_{start}")
            function = TANH if g == GATE_CANDIDATE else SIGMOID
            nc.scalar.activation(gate[:], pre[g, start][:], function, bias=bias[:, g : g + 1])
            return {(lo, hi): gate[:, lo - start : hi - start] for lo, hi in PARTS[piece]}

        cell = {}
        tanh_cell = {}

        def new_cell_state(piece, bias):
            squashed = {}
            for g in CELL_GATES[piece]:
                squashed[g] = squash(g, piece, bias)
            fresh = {}
            kept = {}

            def multiply_input_and_candidate():
                for lo, hi in PARTS[piece]:
                    fresh[lo] = held.tile([P, hi - lo], F32, name=f"fresh{lo}")
                    nc.vector.tensor_tensor(fresh[lo][:], squashed[GATE_IN][lo, hi], squashed[GATE_CANDIDATE][lo, hi], MULT)

            def multiply_forget_and_old_state():
                for lo, hi in PARTS[piece]:
                    kept[lo] = held.tile([P, hi - lo], F32, name=f"kept{lo}")
                    nc.vector.tensor_tensor(kept[lo][:], squashed[GATE_FORGET][lo, hi], columns(c0_sb, piece, lo, hi), MULT)

            if CELL_GATES[piece][0] == GATE_FORGET:
                multiply_forget_and_old_state()
                multiply_input_and_candidate()
            else:
                multiply_input_and_candidate()
                multiply_forget_and_old_state()
            start, end = piece
            cell[piece] = held.tile([P, end - start], F32, name=f"cell{start}")
            for lo, hi in PARTS[piece]:
                nc.vector.tensor_tensor(cell[piece][:, lo - start : hi - start], kept[lo][:], fresh[lo][:], ADD)

        def copy_bias_behind_cell_state(piece):
            copied = held.tile([P, GATES], F32, name=f"bias_behind{piece[0]}", tag=f"kept{PARTS[piece][-1][0]}")
            nc.vector.tensor_copy(copied[:], bias_sb[:])
            return copied

        def tanh_of_cell(piece):
            start, end = piece
            tanh_cell[piece] = held.tile([P, end - start], F32, name=f"tanh_cell{start}")
            for lo, hi in PARTS[piece] if piece == THIRD else (piece,):
                columns_of_part = slice(lo - start, hi - start)
                nc.scalar.activation(tanh_cell[piece][:, columns_of_part], cell[piece][:, columns_of_part], TANH)

        def new_hidden_state(gate_out, piece):
            start = piece[0]
            for lo, hi in PARTS[piece]:
                hidden = held.tile([P, hi - lo], F32, name=f"hidden{lo}")
                nc.vector.tensor_tensor(hidden[:], gate_out[lo, hi], tanh_cell[piece][:, lo - start : hi - start], MULT)
                nc.sync.dma_start(out[:, lo:hi], hidden[:])

        for repeat in range(WARM_UP_MATMULS):
            nc.tensor.matmul(pre[CELL_GATES[THIRD][0], THIRD[0]][:, 0:P], zeros[:], zeros[:], start=True, stop=True)

        for g in CELL_GATES[FIRST] + (GATE_OUT,):
            plain_products(g, *FIRST, opens=True, width=PIECE)
        for g in CELL_GATES[FIRST]:
            looked_up_product(g, *FIRST, opens=False)
        for g in CELL_GATES[SECOND]:
            looked_up_product(g, *SECOND, opens=True)
        new_cell_state(FIRST, bias_sb)
        bias_behind_first = copy_bias_behind_cell_state(FIRST)
        tanh_of_cell(FIRST)

        for g in CELL_GATES[SECOND]:
            plain_products(g, *SECOND, opens=False, width=NARROW)
        new_cell_state(SECOND, bias_sb)
        bias_behind_second = copy_bias_behind_cell_state(SECOND)

        open_bank(CELL_GATES[THIRD][1], THIRD, successor_of=(CELL_GATES[FIRST][0], FIRST))
        open_bank(CELL_GATES[THIRD][2], THIRD, successor_of=(CELL_GATES[FIRST][1], FIRST))
        for g in CELL_GATES[THIRD]:
            plain_products(g, *THIRD, opens=True, width=NARROW)
        for g in CELL_GATES[THIRD]:
            looked_up_product(g, *THIRD, opens=False)
        new_cell_state(THIRD, bias_behind_first)

        open_bank(GATE_OUT, SECOND, successor_of=(CELL_GATES[FIRST][2], FIRST))
        open_bank(GATE_OUT, THIRD, successor_of=(CELL_GATES[SECOND][0], SECOND))
        looked_up_product(GATE_OUT, *FIRST, opens=False)
        for piece in (SECOND, THIRD):
            looked_up_product(GATE_OUT, *piece, opens=True)
        for piece in (SECOND, THIRD):
            plain_products(GATE_OUT, *piece, opens=False, width=PIECE // 2)
        tanh_of_cell(SECOND)
        new_hidden_state(squash(GATE_OUT, FIRST, bias_behind_second), FIRST)
        tanh_of_cell(THIRD)
        new_hidden_state(squash(GATE_OUT, SECOND, bias_behind_second), SECOND)
        new_hidden_state(squash(GATE_OUT, THIRD, bias_behind_second), THIRD)
